import numpy as np
import ml_dtypes

BF16 = ml_dtypes.bfloat16


def bf(x):
    return np.asarray(x, np.float32).astype(BF16)


def f32(x):
    return np.asarray(x, np.float32)


def f64(x):
    return np.asarray(x).astype(np.float64)


def striped(idx):
    return np.tile(idx.reshape(-1, 16).T, (8, 1))


C, S, N, M = 256, 425, 768, 128
TEMP = 1000.0


def sinusoid():
    pos = np.arange(S)[:, None].astype(np.float64)
    i = np.arange(C)[None, :]
    angle = pos / np.power(TEMP, 2 * (i // 2) / C)
    return np.ascontiguousarray(np.where(i % 2 == 0, np.sin(angle), np.cos(angle)).T)


def setup_inputs():
    return {"pos_table": f32(sinusoid()), "u": f32(np.random.standard_normal((C, N))), "wq": bf(0.05 * np.random.standard_normal((C, M))), "bq": f32(0.1 * np.random.standard_normal((M, 1))), "wk": bf(0.05 * np.random.standard_normal((C, M))), "bk": f32(0.1 * np.random.standard_normal((M, 1))), "offs": striped(np.random.permutation(np.tile(np.arange(S), 2))[:N])}


def reference(pos_table, u, wq, bq, wk, bk, offs):
    idx = offs[:16].T.reshape(-1)
    e = f64(pos_table)[:, idx] + np.maximum(f64(u), 0.0)
    q = f64(wq).T @ e + f64(bq)
    k = f64(wk).T @ e + f64(bk)
    return np.concatenate([e, q, k], axis=0)

@@ -1,0 +1,77 @@
+import concourse.mybir as mybir
+
+F32 = mybir.dt.float32
+BF16 = mybir.dt.bfloat16
+U16 = mybir.dt.uint16
+ADD = mybir.AluOpType.add
+RELU = mybir.ActivationFunctionType.Relu
+IDENTITY = mybir.ActivationFunctionType.Identity
+
+P = 128
+C, S, N, M = 256, 425, 768, 128
+BLOCKS = C // P
+PIECE = 192
+PIECES = N // PIECE
+OFFSET_COLUMNS = PIECE // 16
+
+FLOPS = 2 * C * (2 * M) * N
+
+
+def tile_unite_kernel(tc, pos_table, u, wq, bq, wk, bk, offs, out):
+    nc = tc.nc
+
+    u_view = u.rearrange("(b p) n -> p b n", p=P)
+    e_view = out[0:C, :].rearrange("(b p) n -> p b n", p=P)
+    qk_view = out[C : C + 2 * M, :].rearrange("(t p) n -> p t n", p=P)
+
+    with (
+        tc.tile_pool(name="held", bufs=1) as held,
+        tc.tile_pool(name="pieces", bufs=PIECES) as pieces,
+        tc.psum_pool(name="psum", bufs=4) as psum,
+    ):
+        offsets = held.tile([P, N // 16], U16, name="offsets")
+        nc.sync.dma_start(offsets[:], offs)
+
+        tables = []
+        for b in range(BLOCKS):
+            table = held.tile([P, S], F32, name=f"table{b}")
+            nc.sync.dma_start(table[:], pos_table[b * P : (b + 1) * P, :])
+            tables.append(table)
+
+        weights = []
+        for name, w, bias in (("q", wq, bq), ("k", wk, bk)):
+            w_sb = held.tile([P, BLOCKS, M], BF16, name=f"w{name}_sb")
+            nc.gpsimd.dma_start(w_sb[:], w.rearrange("(b p) m -> p b m", p=P))
+            bias_sb = held.tile([P, 1], F32, name=f"b{name}_sb")
+            nc.gpsimd.dma_start(bias_sb[:], bias)
+            weights.append((w_sb, bias_sb))
+
+        activated = []
+        for j in range(PIECES):
+            columns = slice(j * PIECE, (j + 1) * PIECE)
+            r = pieces.tile([P, BLOCKS, PIECE], F32, name="r")
+            nc.scalar.dma_start(r[:], u_view[:, :, columns])
+            nc.scalar.activation(r[:], r[:], RELU)
+            activated.append(r)
+
+        for j in range(PIECES):
+            columns = slice(j * PIECE, (j + 1) * PIECE)
+            piece_offsets = offsets[:, j * OFFSET_COLUMNS : (j + 1) * OFFSET_COLUMNS]
+            r = activated[j]
+
+            e = pieces.tile([P, BLOCKS, PIECE], F32, name="e")
+            e_bf = pieces.tile([P, BLOCKS, PIECE], BF16, name="e_bf")
+            for b in range(BLOCKS):
+                nc.vector.tensor_tensor(e[:, b, :], tables[b][:].indirect(piece_offsets), r[:, b, :], ADD)
+                nc.vector.tensor_copy(e_bf[:, b, :], e[:, b, :])
+            nc.sync.dma_start(e_view[:, :, columns], e[:])
+
+            qk = pieces.tile([P, 2, PIECE], F32, name="qk")
+            for t, (w_sb, bias_sb) in enumerate(weights):
+                product = psum.tile([P, PIECE], F32, name="product")
+                for b in range(BLOCKS):
+                    nc.tensor.matmul(
+                        product[:], w_sb[:, b, :], e_bf[:, b, :], start=(b == 0), stop=(b == BLOCKS - 1)
+                    )
+                nc.scalar.activation(qk[:, t, :], product[:], IDENTITY, bias=bias_sb[:])
+            nc.sync.dma_start(qk_view[:, :, columns], qk[:])

@@ -64,7 +64,7 @@ def tile_unite_kernel(tc, pos_table, u, wq, bq, wk, bk, offs, out):
             for b in range(BLOCKS):
                 nc.vector.tensor_tensor(e[:, b, :], tables[b][:].indirect(piece_offsets), r[:, b, :], ADD)
                 nc.vector.tensor_copy(e_bf[:, b, :], e[:, b, :])
-            nc.sync.dma_start(e_view[:, :, columns], e[:])
+            nc.gpsimd.dma_start(e_view[:, :, columns], e[:])
 
             qk = pieces.tile([P, 2, PIECE], F32, name="qk")
             for t, (w_sb, bias_sb) in enumerate(weights):

@@ -10,8 +10,10 @@ IDENTITY = mybir.ActivationFunctionType.Identity
 P = 128
 C, S, N, M = 256, 425, 768, 128
 BLOCKS = C // P
+HALVES = 2
+HALF = N // HALVES
 PIECE = 192
-PIECES = N // PIECE
+PIECES = HALF // PIECE
 OFFSET_COLUMNS = PIECE // 16
 
 FLOPS = 2 * C * (2 * M) * N
@@ -20,14 +22,14 @@ FLOPS = 2 * C * (2 * M) * N
 def tile_unite_kernel(tc, pos_table, u, wq, bq, wk, bk, offs, out):
     nc = tc.nc
 
-    u_view = u.rearrange("(b p) n -> p b n", p=P)
-    e_view = out[0:C, :].rearrange("(b p) n -> p b n", p=P)
+    table_view = pos_table.rearrange("(p b) s -> p b s", b=BLOCKS)
+    u_view = u.rearrange("(p b) n -> p b n", b=BLOCKS)
+    e_view = out[0:C, :].rearrange("(p b) n -> p b n", b=BLOCKS)
     qk_view = out[C : C + 2 * M, :].rearrange("(t p) n -> p t n", p=P)
 
     with (
         tc.tile_pool(name="held", bufs=1) as held,
-        tc.tile_pool(name="pieces", bufs=PIECES) as pieces,
-        tc.psum_pool(name="psum", bufs=4) as psum,
+        tc.psum_pool(name="psum", bufs=2 * HALVES * PIECES) as psum,
     ):
         offsets = held.tile([P, N // 16], U16, name="offsets")
         nc.sync.dma_start(offsets[:], offs)
@@ -35,43 +37,57 @@ def tile_unite_kernel(tc, pos_table, u, wq, bq, wk, bk, offs, out):
         tables = []
         for b in range(BLOCKS):
             table = held.tile([P, S], F32, name=f"table{b}")
-            nc.sync.dma_start(table[:], pos_table[b * P : (b + 1) * P, :])
+            nc.sync.dma_start(table[:], table_view[:, b, :])
             tables.append(table)
+
+        u_halves = [held.tile([P, BLOCKS, HALF], F32, name=f"u_half{h}") for h in range(HALVES)]
+        for b in range(BLOCKS):
+            nc.scalar.dma_start(u_halves[0][:, b, :], u_view[:, b, 0:HALF])
+        nc.sync.dma_start(u_halves[1][:], u_view[:, :, HALF:N])
 
         weights = []
         for name, w, bias in (("q", wq, bq), ("k", wk, bk)):
             w_sb = held.tile([P, BLOCKS, M], BF16, name=f"w{name}_sb")
-            nc.gpsimd.dma_start(w_sb[:], w.rearrange("(b p) m -> p b m", p=P))
+            nc.scalar.dma_start(w_sb[:], w.rearrange("(p b) m -> p b m", b=BLOCKS))
             bias_sb = held.tile([P, 1], F32, name=f"b{name}_sb")
             nc.gpsimd.dma_start(bias_sb[:], bias)
             weights.append((w_sb, bias_sb))
 
-        activated = []
-        for j in range(PIECES):
-            columns = slice(j * PIECE, (j + 1) * PIECE)
-            r = pieces.tile([P, BLOCKS, PIECE], F32, name="r")
-            nc.scalar.dma_start(r[:], u_view[:, :, columns])
-            nc.scalar.activation(r[:], r[:], RELU)
-            activated.append(r)
-
-        for j in range(PIECES):
-            columns = slice(j * PIECE, (j + 1) * PIECE)
-            piece_offsets = offsets[:, j * OFFSET_COLUMNS : (j + 1) * OFFSET_COLUMNS]
-            r = activated[j]
-
-            e = pieces.tile([P, BLOCKS, PIECE], F32, name="e")
-            e_bf = pieces.tile([P, BLOCKS, PIECE], BF16, name="e_bf")
+        for r in u_halves:
             for b in range(BLOCKS):
-                nc.vector.tensor_tensor(e[:, b, :], tables[b][:].indirect(piece_offsets), r[:, b, :], ADD)
-                nc.vector.tensor_copy(e_bf[:, b, :], e[:, b, :])
-            nc.gpsimd.dma_start(e_view[:, :, columns], e[:])
+                for j in range(PIECES):
+                    piece = r[:, b, j * PIECE : (j + 1) * PIECE]
+                    nc.scalar.activation(piece, piece, RELU)
 
-            qk = pieces.tile([P, 2, PIECE], F32, name="qk")
-            for t, (w_sb, bias_sb) in enumerate(weights):
-                product = psum.tile([P, PIECE], F32, name="product")
-                for b in range(BLOCKS):
-                    nc.tensor.matmul(
-                        product[:], w_sb[:, b, :], e_bf[:, b, :], start=(b == 0), stop=(b == BLOCKS - 1)
+        for h in range(HALVES):
+            r = u_halves[h]
+            e = held.tile([P, BLOCKS, HALF], F32, name=f"e{h}")
+            e_bf = held.tile([P, BLOCKS, HALF], BF16, name=f"e_bf{h}")
+            qk = held.tile([P, 2, HALF], F32, name=f"qk{h}")
+            products = [
+                [psum.tile([P, PIECE], F32, name=f"product{h}{j}{t}", tag="product") for t in range(2)]
+                for j in range(PIECES)
+            ]
+            for b in range(BLOCKS):
+                for j in range(PIECES):
+                    columns = slice(j * PIECE, (j + 1) * PIECE)
+                    first = (h * PIECES + j) * OFFSET_COLUMNS
+                    piece_offsets = offsets[:, first : first + OFFSET_COLUMNS]
+
+                    nc.vector.tensor_tensor(
+                        e[:, b, columns], tables[b][:].indirect(piece_offsets), r[:, b, columns], ADD
                     )
-                nc.scalar.activation(qk[:, t, :], product[:], IDENTITY, bias=bias_sb[:])
-            nc.sync.dma_start(qk_view[:, :, columns], qk[:])
+                    nc.vector.tensor_copy(e_bf[:, b, columns], e[:, b, columns])
+
+                    for t, (w_sb, bias_sb) in enumerate(weights):
+                        product = products[j][t]
+                        nc.tensor.matmul(
+                            product[:], w_sb[:, b, :], e_bf[:, b, columns], start=(b == 0), stop=(b == BLOCKS - 1)
+                        )
+                        if b == BLOCKS - 1:
+                            nc.scalar.activation(qk[:, t, columns], product[:], IDENTITY, bias=bias_sb[:])
+                    if b == BLOCKS - 1 and h == HALVES - 1:
+                        nc.sync.dma_start(qk_view[:, :, h * HALF + j * PIECE : h * HALF + (j + 1) * PIECE], qk[:, :, columns])
+                nc.sync.dma_start(e_view[:, b, h * HALF : (h + 1) * HALF], e[:, b, :])
+            if h < HALVES - 1:
+                nc.sync.dma_start(qk_view[:, :, h * HALF : (h + 1) * HALF], qk[:])

@@ -85,9 +85,14 @@ def tile_unite_kernel(tc, pos_table, u, wq, bq, wk, bk, offs, out):
                             product[:], w_sb[:, b, :], e_bf[:, b, columns], start=(b == 0), stop=(b == BLOCKS - 1)
                         )
                         if b == BLOCKS - 1:
-                            nc.scalar.activation(qk[:, t, columns], product[:], IDENTITY, bias=bias_sb[:])
+                            if h == HALVES - 1 and t == 1:
+                                nc.vector.tensor_scalar_add(qk[:, t, columns], product[:], bias_sb[:])
+                            else:
+                                nc.scalar.activation(qk[:, t, columns], product[:], IDENTITY, bias=bias_sb[:])
                     if b == BLOCKS - 1 and h == HALVES - 1:
                         nc.sync.dma_start(qk_view[:, :, h * HALF + j * PIECE : h * HALF + (j + 1) * PIECE], qk[:, :, columns])
-                nc.sync.dma_start(e_view[:, b, h * HALF : (h + 1) * HALF], e[:, b, :])
+                last = h == HALVES - 1 and b == BLOCKS - 1
+                queue = nc.scalar if last else nc.sync
+                queue.dma_start(e_view[:, b, h * HALF : (h + 1) * HALF], e[:, b, :])
             if h < HALVES - 1:
                 nc.sync.dma_start(qk_view[:, :, h * HALF : (h + 1) * HALF], qk[:])

import concourse.mybir as mybir

F32 = mybir.dt.float32
BF16 = mybir.dt.bfloat16
U16 = mybir.dt.uint16
ADD = mybir.AluOpType.add
RELU = mybir.ActivationFunctionType.Relu
IDENTITY = mybir.ActivationFunctionType.Identity

P = 128
C, S, N, M = 256, 425, 768, 128
BLOCKS = C // P
HALVES = 2
HALF = N // HALVES
PIECE = 192
PIECES = HALF // PIECE
OFFSET_COLUMNS = PIECE // 16

FLOPS = 2 * C * (2 * M) * N


def tile_unite_kernel(tc, pos_table, u, wq, bq, wk, bk, offs, out):
    nc = tc.nc

    table_view = pos_table.rearrange("(p b) s -> p b s", b=BLOCKS)
    u_view = u.rearrange("(p b) n -> p b n", b=BLOCKS)
    e_view = out[0:C, :].rearrange("(p b) n -> p b n", b=BLOCKS)
    qk_view = out[C : C + 2 * M, :].rearrange("(t p) n -> p t n", p=P)

    with (
        tc.tile_pool(name="held", bufs=1) as held,
        tc.psum_pool(name="psum", bufs=2 * HALVES * PIECES) as psum,
    ):
        offsets = held.tile([P, N // 16], U16, name="offsets")
        nc.sync.dma_start(offsets[:], offs)

        tables = []
        for b in range(BLOCKS):
            table = held.tile([P, S], F32, name=f"table{b}")
            nc.sync.dma_start(table[:], table_view[:, b, :])
            tables.append(table)

        u_halves = [held.tile([P, BLOCKS, HALF], F32, name=f"u_half{h}") for h in range(HALVES)]
        for b in range(BLOCKS):
            nc.scalar.dma_start(u_halves[0][:, b, :], u_view[:, b, 0:HALF])
        nc.sync.dma_start(u_halves[1][:], u_view[:, :, HALF:N])

        weights = []
        for name, w, bias in (("q", wq, bq), ("k", wk, bk)):
            w_sb = held.tile([P, BLOCKS, M], BF16, name=f"w{name}_sb")
            nc.scalar.dma_start(w_sb[:], w.rearrange("(p b) m -> p b m", b=BLOCKS))
            bias_sb = held.tile([P, 1], F32, name=f"b{name}_sb")
            nc.gpsimd.dma_start(bias_sb[:], bias)
            weights.append((w_sb, bias_sb))

        for r in u_halves:
            for b in range(BLOCKS):
                for j in range(PIECES):
                    piece = r[:, b, j * PIECE : (j + 1) * PIECE]
                    nc.scalar.activation(piece, piece, RELU)

        for h in range(HALVES):
            r = u_halves[h]
            e = held.tile([P, BLOCKS, HALF], F32, name=f"e{h}")
            e_bf = held.tile([P, BLOCKS, HALF], BF16, name=f"e_bf{h}")
            qk = held.tile([P, 2, HALF], F32, name=f"qk{h}")
            products = [
                [psum.tile([P, PIECE], F32, name=f"product{h}{j}{t}", tag="product") for t in range(2)]
                for j in range(PIECES)
            ]
            for b in range(BLOCKS):
                for j in range(PIECES):
                    columns = slice(j * PIECE, (j + 1) * PIECE)
                    first = (h * PIECES + j) * OFFSET_COLUMNS
                    piece_offsets = offsets[:, first : first + OFFSET_COLUMNS]

                    nc.vector.tensor_tensor(
                        e[:, b, columns], tables[b][:].indirect(piece_offsets), r[:, b, columns], ADD
                    )
                    nc.vector.tensor_copy(e_bf[:, b, columns], e[:, b, columns])

                    for t, (w_sb, bias_sb) in enumerate(weights):
                        product = products[j][t]
                        nc.tensor.matmul(
                            product[:], w_sb[:, b, :], e_bf[:, b, columns], start=(b == 0), stop=(b == BLOCKS - 1)
                        )
                        if b == BLOCKS - 1:
                            if h == HALVES - 1 and t == 1:
                                nc.vector.tensor_scalar_add(qk[:, t, columns], product[:], bias_sb[:])
                            else:
                                nc.scalar.activation(qk[:, t, columns], product[:], IDENTITY, bias=bias_sb[:])
                    if b == BLOCKS - 1 and h == HALVES - 1:
                        nc.sync.dma_start(qk_view[:, :, h * HALF + j * PIECE : h * HALF + (j + 1) * PIECE], qk[:, :, columns])
                last = h == HALVES - 1 and b == BLOCKS - 1
                queue = nc.scalar if last else nc.sync
                queue.dma_start(e_view[:, b, h * HALF : (h + 1) * HALF], e[:, b, :])
            if h < HALVES - 1:
                nc.sync.dma_start(qk_view[:, :, h * HALF : (h + 1) * HALF], qk[:])
